import numpy as np
import ml_dtypes


def mxq(x, axis, fmt="e4m3"):
    dtype, down = {"e4m3": (ml_dtypes.float8_e4m3fn, 7), "e5m2": (ml_dtypes.float8_e5m2, 14)}[fmt]
    v = np.moveaxis(np.asarray(x, np.float32).astype(ml_dtypes.bfloat16).astype(np.float64), axis, -1)
    blocks = v.reshape(v.shape[:-1] + (-1, 32))
    amax = np.abs(blocks).max(-1, keepdims=True)
    byte = np.maximum(np.where(amax > 0, np.frexp(amax)[1] - 1 + 127, 0) - down, 1)
    scale = np.exp2(byte - 127.0)
    codes = (blocks / scale).astype(np.float32).astype(dtype).astype(np.float64)
    return np.moveaxis((codes * scale).reshape(v.shape), -1, axis)


WIDE = False


def mx_kscale(k):
    if not WIDE:
        return np.ones(k)
    levels = np.array([10, -10, 5, -5, 0])
    a = np.random.permutation(np.resize(levels, k // 512 * 4)).reshape(k // 512, 4)
    idx = np.arange(k)
    return np.exp2(a[idx // 512, idx % 128 // 32])


BF16 = ml_dtypes.bfloat16


def bf(x):
    return np.asarray(x, np.float32).astype(BF16)


def f64(x):
    return np.asarray(x).astype(np.float64)


E2M1 = np.array([0.0, 0.5, 1.0, 1.5, 2.0, 3.0, 4.0, 6.0, -0.0, -0.5, -1.0, -1.5, -2.0, -3.0, -4.0, -6.0])


def pack_weight(w, fmt):
    k, n = w.shape
    w = f64(bf(w)).reshape(k // 32, 32, n)
    amax = np.abs(w).max(1)
    if fmt == "e4m3":
        byte = np.frexp(amax)[1] - 1 + 127 - 7
    else:
        mant, ex = np.frexp(amax / 6.0)
        byte = np.where(mant > 0.5, ex, ex - 1) + 127
    byte = np.clip(np.where(amax > 0, byte, 1), 1, 254)
    scaled = (w * np.exp2(127.0 - byte)[:, None, :]).reshape(k, n).astype(np.float32)
    by_word = np.ascontiguousarray(scaled.reshape(k // 512, 128, 4, n).transpose(0, 1, 3, 2))
    if fmt == "e4m3":
        words = by_word.astype(ml_dtypes.float8_e4m3fn).view(np.uint8)
    else:
        c = by_word.astype(ml_dtypes.float4_e2m1fn).view(np.uint8) & 0xF
        words = c[..., 0::2] | (c[..., 1::2] << 4)
    return np.ascontiguousarray(words), np.ascontiguousarray(byte.astype(np.uint8).reshape(k // 512, 16, n))


def unpack_weight(words, scales, fmt):
    g, p, n, _ = words.shape
    if fmt == "e4m3":
        vals = np.ascontiguousarray(words).view(ml_dtypes.float8_e4m3fn).astype(np.float64)
    else:
        nib = np.empty((g, p, n, 4), np.uint8)
        nib[..., 0::2] = words & 0xF
        nib[..., 1::2] = words >> 4
        vals = E2M1[nib]
    vals = vals * np.repeat(np.exp2(scales.astype(np.float64) - 127.0), 8, axis=1)[..., None]
    return vals.transpose(0, 1, 3, 2).reshape(g * 512, n)

def pack4(w):
    words, scales = pack_weight(w, "e2m1")
    return words.reshape(words.shape[0], 128, -1), scales


def unpack4(words, scales):
    return unpack_weight(words.reshape(words.shape[0], 128, -1, 2), scales, "e2m1")


E, D_NODE, D_EDGE, D_GLOB, LATENT, D_OUT = 4096, 128, 128, 128, 512, 128
D_IN = D_NODE + D_NODE + D_EDGE + D_GLOB


def setup_inputs():
    s = mx_kscale(D_IN)
    o1 = D_NODE
    o2 = o1 + D_NODE
    o3 = o2 + D_EDGE
    receiver = bf(np.random.standard_normal((E, D_NODE)) * s[:o1])
    sender = bf(np.random.standard_normal((E, D_NODE)) * s[o1:o2])
    edge_attr = bf(np.random.standard_normal((E, D_EDGE)) * s[o2:o3])
    global_attr = bf(np.random.standard_normal((1, D_GLOB)) * s[o3:])
    W1_words, W1_scales = pack4(np.random.standard_normal((D_IN, LATENT)) / np.sqrt(D_IN) / s[:, None])
    b1 = bf(np.random.standard_normal(LATENT) * 0.1)
    return {
        "receiver": receiver,
        "sender": sender,
        "edge_attr": edge_attr,
        "global_attr": global_attr,
        "W1_words": W1_words,
        "W1_scales": W1_scales,
        "b1": b1,
    }


def reference(receiver, sender, edge_attr, global_attr, W1_words, W1_scales, b1):
    e = edge_attr.shape[0]
    g = np.tile(f64(global_attr), (e // global_attr.shape[0], 1))
    x = np.concatenate([f64(receiver), f64(sender), f64(edge_attr), g], axis=1)
    return np.maximum((mxq(x, 1, "e4m3") @ unpack4(W1_words, W1_scales)) + f64(b1), 0.0)

@@ -1,0 +1,169 @@
+import concourse.mybir as mybir
+from concourse.masks import make_identity
+
+FLOPS = 2 * 4096 * 512 * 512
+
+BF16 = mybir.dt.bfloat16
+F32 = mybir.dt.float32
+I32 = mybir.dt.int32
+U8 = mybir.dt.uint8
+U32 = mybir.dt.uint32
+FP8X4 = mybir.dt.float8_e4m3fn_x4
+FP4X4 = mybir.dt.float4_e2m1fn_x4
+ALU = mybir.AluOpType
+ACT = mybir.ActivationFunctionType
+
+P = 128
+EDGES = 4096
+TILES = EDGES // P
+FEATURES = 128
+QUADRANT = FEATURES // 4
+LATENT = 512
+PAIR = 2
+PAIRS = TILES // PAIR
+CHUNK = 4
+CHUNKS = TILES // CHUNK
+LARGEST_F32 = 3.4028234663852886e38
+SCALAR_RELU_EVERY = 4
+
+
+def tile_edgemodel_pa_kernel(
+    tc, receiver, sender, edge_attr, global_attr, W1_words, W1_scales, b1, out
+):
+    nc = tc.nc
+    streams = [
+        piece.rearrange("(p j) k -> p j k", j=TILES) for piece in (receiver, sender, edge_attr)
+    ]
+    out_rows = out.rearrange("(p j) n -> p j n", j=TILES)
+
+    with (
+        tc.tile_pool(name="keep", bufs=1) as keep,
+        tc.psum_pool(name="planes", bufs=2) as planes_pool,
+        tc.psum_pool(name="sums", bufs=6) as sums_pool,
+        tc.manual_schedule(),
+    ):
+        identity = keep.tile([P, P], F32)
+        w_words = keep.tile([P, 2 * LATENT], U8, align_bytes=64)
+        w_scales = keep.tile([P, LATENT], U8, align_bytes=64)
+        bias = keep.tile([P, LATENT], BF16)
+        global_rows = keep.tile([P, FEATURES], BF16)
+        table_warmer = keep.tile([P, 1], F32)
+        loaded = [
+            keep.tile([P, TILES, FEATURES], BF16, name="loaded_%d" % s) for s in range(len(streams))
+        ]
+        x_words = keep.tile([P, TILES, 2, P], F32)
+        x_grouped = keep.tile([P, TILES, 4 * P], BF16, align_bytes=64)
+        x_codes = keep.tile([P, TILES, P], U32, align_bytes=64)
+        x_scales = keep.tile([P, TILES, P], U8, align_bytes=64)
+        result = keep.tile([P, TILES, LATENT], F32)
+        sums = {}
+
+        def load_chunk(c):
+            tiles = slice(c * CHUNK, (c + 1) * CHUNK)
+            for s, stream in enumerate(streams):
+                nc.sync.dma_start(out=loaded[s][:, tiles, :], in_=stream[:, tiles, :])
+
+        def sort_chunk(c):
+            tiles = slice(c * CHUNK, (c + 1) * CHUNK)
+            for s in range(len(streams)):
+                nc.scalar.copy(
+                    out=x_words[:, tiles, :, s * QUADRANT : (s + 1) * QUADRANT],
+                    in_=loaded[s][:, tiles, :].bitcast(F32).rearrange("p j (q u) -> p j u q", u=2),
+                )
+
+        def repeat_global(first, last):
+            nc.vector.tensor_copy(
+                out=x_words[:, first:last, :, 3 * QUADRANT :],
+                in_=global_rows[:]
+                .bitcast(F32)
+                .rearrange("p (q u) -> p u q", u=2)
+                .unsqueeze(1)
+                .to_broadcast([P, last - first, 2, QUADRANT]),
+            )
+
+        def transpose_pair(i):
+            tiles = slice(i * PAIR, (i + 1) * PAIR)
+            planes = planes_pool.tile([P, PAIR, 2, P], F32)
+            for jj in range(PAIR):
+                for u in range(2):
+                    nc.tensor.transpose(planes[:, jj, u, :], x_words[:, i * PAIR + jj, u, :], identity[:])
+            nc.scalar.copy(
+                out=x_grouped[:, tiles, :].bitcast(F32).rearrange("p j (e u) -> p j e u", u=2),
+                in_=planes[:].rearrange("p j u e -> p j e u"),
+            )
+
+        def quantise_pair(i):
+            tiles = slice(i * PAIR, (i + 1) * PAIR)
+            nc.vector.quantize_mx(
+                out=x_codes[:, tiles, :].rearrange("p j e -> p (j e)").bitcast(FP8X4),
+                scales=x_scales[:, tiles, :].rearrange("p j e -> p (j e)"),
+                in_=x_grouped[:, tiles, :].rearrange("p j c -> p (j c)"),
+            )
+
+        def multiply_pair(i):
+            for j in range(i * PAIR, (i + 1) * PAIR):
+                acc = sums_pool.tile([P, LATENT], F32)
+                nc.tensor.matmul_mx(
+                    out=acc[:],
+                    lhsT=x_codes[:, j, :].bitcast(FP8X4),
+                    lhsT_scale=x_scales[:, j, :],
+                    rhs=w_words[:].bitcast(FP4X4),
+                    rhs_scale=w_scales[:],
+                    start=True,
+                    stop=True,
+                )
+                sums[j] = acc
+
+        def add_bias_pair(i):
+            for j in range(i * PAIR, (i + 1) * PAIR):
+                nc.vector.tensor_tensor(out=result[:, j, :], in0=sums[j][:], in1=bias[:], op=ALU.add)
+
+        def relu_and_store_pair(i):
+            tiles = slice(i * PAIR, (i + 1) * PAIR)
+            if i % SCALAR_RELU_EVERY == SCALAR_RELU_EVERY - 1:
+                nc.scalar.activation(out=result[:, tiles, :], in_=result[:, tiles, :], func=ACT.Relu)
+            else:
+                nc.gpsimd.tensor_scalar(
+                    out=result[:, tiles, :],
+                    in0=result[:, tiles, :],
+                    scalar1=LARGEST_F32,
+                    scalar2=0.0,
+                    op0=ALU.min,
+                    op1=ALU.max,
+                )
+            nc.sync.dma_start(out=out_rows[:, tiles, :], in_=result[:, tiles, :])
+
+        nc.scalar.dma_start(
+            out=global_rows[:], in_=global_attr.rearrange("o k -> (o k)").partition_broadcast(P)
+        )
+        nc.scalar.dma_start(out=bias[:], in_=b1.partition_broadcast(P))
+        load_chunk(0)
+        nc.sync.dma_start(out=w_words[:].bitcast(I32), in_=W1_words[0].bitcast(I32))
+        nc.vector.memset(w_scales[:].bitcast(I32), 0)
+        for quadrant in range(4):
+            nc.sync.dma_start(
+                out=w_scales[32 * quadrant : 32 * quadrant + 4, :].bitcast(I32),
+                in_=W1_scales[0, 4 * quadrant : 4 * quadrant + 4, :].bitcast(I32),
+            )
+        for c in range(1, CHUNKS):
+            load_chunk(c)
+
+        make_identity(nc, identity[:])
+        nc.vector.memset(table_warmer[:], 0.0)
+        nc.scalar.activation(out=table_warmer[:], in_=table_warmer[:], func=ACT.Relu)
+        repeat_global(0, CHUNK)
+        repeat_global(CHUNK, TILES)
+
+        sort_chunk(0)
+        for step in range(PAIRS + 3):
+            if step < PAIRS:
+                transpose_pair(step)
+                if step % (CHUNK // PAIR) == 0 and step // (CHUNK // PAIR) + 1 < CHUNKS:
+                    sort_chunk(step // (CHUNK // PAIR) + 1)
+            if 0 <= step - 1 < PAIRS:
+                quantise_pair(step - 1)
+                multiply_pair(step - 1)
+            if 0 <= step - 2 < PAIRS:
+                add_bias_pair(step - 2)
+            if 0 <= step - 3 < PAIRS:
+                relu_and_store_pair(step - 3)

@@ -24,7 +24,6 @@ PAIRS = TILES // PAIR
 CHUNK = 4
 CHUNKS = TILES // CHUNK
 LARGEST_F32 = 3.4028234663852886e38
-SCALAR_RELU_EVERY = 4
 
 
 def tile_edgemodel_pa_kernel(
@@ -120,8 +119,10 @@ def tile_edgemodel_pa_kernel(
 
         def relu_and_store_pair(i):
             tiles = slice(i * PAIR, (i + 1) * PAIR)
-            if i % SCALAR_RELU_EVERY == SCALAR_RELU_EVERY - 1:
+            if i % 2 == 0:
                 nc.scalar.activation(out=result[:, tiles, :], in_=result[:, tiles, :], func=ACT.Relu)
+            elif i % 4 == 3:
+                nc.vector.tensor_scalar_max(out=result[:, tiles, :], in0=result[:, tiles, :], scalar1=0.0)
             else:
                 nc.gpsimd.tensor_scalar(
                     out=result[:, tiles, :],

@@ -23,6 +23,9 @@ PAIR = 2
 PAIRS = TILES // PAIR
 CHUNK = 4
 CHUNKS = TILES // CHUNK
+PAIRS_IN_CHUNK = CHUNK // PAIR
+RING = 2
+VECTOR_SORTS = 3
 LARGEST_F32 = 3.4028234663852886e38
 
 
@@ -50,7 +53,7 @@ def tile_edgemodel_pa_kernel(
         loaded = [
             keep.tile([P, TILES, FEATURES], BF16, name="loaded_%d" % s) for s in range(len(streams))
         ]
-        x_words = keep.tile([P, TILES, 2, P], F32)
+        x_words = keep.tile([P, RING, CHUNK, 2, P], F32)
         x_grouped = keep.tile([P, TILES, 4 * P], BF16, align_bytes=64)
         x_codes = keep.tile([P, TILES, P], U32, align_bytes=64)
         x_scales = keep.tile([P, TILES, P], U8, align_bytes=64)
@@ -64,28 +67,22 @@ def tile_edgemodel_pa_kernel(
 
         def sort_chunk(c):
             tiles = slice(c * CHUNK, (c + 1) * CHUNK)
+            copy = nc.vector.tensor_copy if c < VECTOR_SORTS else nc.scalar.copy
             for s in range(len(streams)):
-                nc.scalar.copy(
-                    out=x_words[:, tiles, :, s * QUADRANT : (s + 1) * QUADRANT],
+                copy(
+                    out=x_words[:, c % RING, :, :, s * QUADRANT : (s + 1) * QUADRANT],
                     in_=loaded[s][:, tiles, :].bitcast(F32).rearrange("p j (q u) -> p j u q", u=2),
                 )
-
-        def repeat_global(first, last):
-            nc.vector.tensor_copy(
-                out=x_words[:, first:last, :, 3 * QUADRANT :],
-                in_=global_rows[:]
-                .bitcast(F32)
-                .rearrange("p (q u) -> p u q", u=2)
-                .unsqueeze(1)
-                .to_broadcast([P, last - first, 2, QUADRANT]),
-            )
 
         def transpose_pair(i):
             tiles = slice(i * PAIR, (i + 1) * PAIR)
             planes = planes_pool.tile([P, PAIR, 2, P], F32)
             for jj in range(PAIR):
                 for u in range(2):
-                    nc.tensor.transpose(planes[:, jj, u, :], x_words[:, i * PAIR + jj, u, :], identity[:])
+                    j = i * PAIR + jj
+                    nc.tensor.transpose(
+                        planes[:, jj, u, :], x_words[:, (j // CHUNK) % RING, j % CHUNK, u, :], identity[:]
+                    )
             nc.scalar.copy(
                 out=x_grouped[:, tiles, :].bitcast(F32).rearrange("p j (e u) -> p j e u", u=2),
                 in_=planes[:].rearrange("p j u e -> p j e u"),
@@ -119,10 +116,10 @@ def tile_edgemodel_pa_kernel(
 
         def relu_and_store_pair(i):
             tiles = slice(i * PAIR, (i + 1) * PAIR)
-            if i % 2 == 0:
-                nc.scalar.activation(out=result[:, tiles, :], in_=result[:, tiles, :], func=ACT.Relu)
-            elif i % 4 == 3:
+            if i % 8 == 7:
                 nc.vector.tensor_scalar_max(out=result[:, tiles, :], in0=result[:, tiles, :], scalar1=0.0)
+            elif i % 4 != 0:
+                nc.scalar.activation(out=result[:, tiles, :], in_=result[:, tiles, :], func=ACT.Relu)
             else:
                 nc.gpsimd.tensor_scalar(
                     out=result[:, tiles, :],
@@ -132,7 +129,8 @@ def tile_edgemodel_pa_kernel(
                     op0=ALU.min,
                     op1=ALU.max,
                 )
-            nc.sync.dma_start(out=out_rows[:, tiles, :], in_=result[:, tiles, :])
+            store_queue = nc.gpsimd if i % 4 == 0 else nc.sync
+            store_queue.dma_start(out=out_rows[:, tiles, :], in_=result[:, tiles, :])
 
         nc.scalar.dma_start(
             out=global_rows[:], in_=global_attr.rearrange("o k -> (o k)").partition_broadcast(P)
@@ -152,15 +150,21 @@ def tile_edgemodel_pa_kernel(
         make_identity(nc, identity[:])
         nc.vector.memset(table_warmer[:], 0.0)
         nc.scalar.activation(out=table_warmer[:], in_=table_warmer[:], func=ACT.Relu)
-        repeat_global(0, CHUNK)
-        repeat_global(CHUNK, TILES)
+        nc.vector.tensor_copy(
+            out=x_words[:].rearrange("p r j u q -> p (r j) u q")[:, :, :, 3 * QUADRANT :],
+            in_=global_rows[:]
+            .bitcast(F32)
+            .rearrange("p (q u) -> p u q", u=2)
+            .unsqueeze(1)
+            .to_broadcast([P, RING * CHUNK, 2, QUADRANT]),
+        )
 
         sort_chunk(0)
         for step in range(PAIRS + 3):
             if step < PAIRS:
                 transpose_pair(step)
-                if step % (CHUNK // PAIR) == 0 and step // (CHUNK // PAIR) + 1 < CHUNKS:
-                    sort_chunk(step // (CHUNK // PAIR) + 1)
+                if step % PAIRS_IN_CHUNK == 0 and step // PAIRS_IN_CHUNK + 1 < CHUNKS:
+                    sort_chunk(step // PAIRS_IN_CHUNK + 1)
             if 0 <= step - 1 < PAIRS:
                 quantise_pair(step - 1)
                 multiply_pair(step - 1)

@@ -25,7 +25,7 @@ CHUNK = 4
 CHUNKS = TILES // CHUNK
 PAIRS_IN_CHUNK = CHUNK // PAIR
 RING = 2
-VECTOR_SORTS = 3
+VECTOR_SORTS = 2
 LARGEST_F32 = 3.4028234663852886e38
 
 
@@ -47,7 +47,9 @@ def tile_edgemodel_pa_kernel(
         identity = keep.tile([P, P], F32)
         w_words = keep.tile([P, 2 * LATENT], U8, align_bytes=64)
         w_scales = keep.tile([P, LATENT], U8, align_bytes=64)
-        bias = keep.tile([P, LATENT], BF16)
+        ones = keep.tile([P, P], BF16)
+        small_rows = keep.tile([P, FEATURES + LATENT], BF16)
+        bias = keep.tile([P, LATENT], F32)
         global_rows = keep.tile([P, FEATURES], BF16)
         table_warmer = keep.tile([P, 1], F32)
         loaded = [
@@ -116,9 +118,9 @@ def tile_edgemodel_pa_kernel(
 
         def relu_and_store_pair(i):
             tiles = slice(i * PAIR, (i + 1) * PAIR)
-            if i % 8 == 7:
+            if i % 4 == 3:
                 nc.vector.tensor_scalar_max(out=result[:, tiles, :], in0=result[:, tiles, :], scalar1=0.0)
-            elif i % 4 != 0:
+            elif i % 4 != 1 or i >= PAIRS - 4:
                 nc.scalar.activation(out=result[:, tiles, :], in_=result[:, tiles, :], func=ACT.Relu)
             else:
                 nc.gpsimd.tensor_scalar(
@@ -129,13 +131,11 @@ def tile_edgemodel_pa_kernel(
                     op0=ALU.min,
                     op1=ALU.max,
                 )
-            store_queue = nc.gpsimd if i % 4 == 0 else nc.sync
-            store_queue.dma_start(out=out_rows[:, tiles, :], in_=result[:, tiles, :])
+            nc.sync.dma_start(out=out_rows[:, tiles, :], in_=result[:, tiles, :])
 
-        nc.scalar.dma_start(
-            out=global_rows[:], in_=global_attr.rearrange("o k -> (o k)").partition_broadcast(P)
-        )
-        nc.scalar.dma_start(out=bias[:], in_=b1.partition_broadcast(P))
+        nc.vector.memset(small_rows[:], 0.0)
+        nc.scalar.dma_start(out=small_rows[0:1, :FEATURES], in_=global_attr)
+        nc.scalar.dma_start(out=small_rows[0:1, FEATURES:], in_=b1.rearrange("(o n) -> o n", o=1))
         load_chunk(0)
         nc.sync.dma_start(out=w_words[:].bitcast(I32), in_=W1_words[0].bitcast(I32))
         nc.vector.memset(w_scales[:].bitcast(I32), 0)
@@ -150,7 +150,15 @@ def tile_edgemodel_pa_kernel(
         make_identity(nc, identity[:])
         nc.vector.memset(table_warmer[:], 0.0)
         nc.scalar.activation(out=table_warmer[:], in_=table_warmer[:], func=ACT.Relu)
-        nc.vector.tensor_copy(
+        nc.vector.memset(ones[:], 1.0)
+        global_spread = sums_pool.tile([P, LATENT], F32, name="acc")
+        nc.tensor.matmul(
+            out=global_spread[:, :FEATURES], lhsT=ones[:], rhs=small_rows[:, :FEATURES], start=True, stop=True
+        )
+        nc.scalar.copy(out=global_rows[:], in_=global_spread[:, :FEATURES])
+        bias_spread = sums_pool.tile([P, LATENT], F32, name="acc")
+        nc.tensor.matmul(out=bias_spread[:], lhsT=ones[:], rhs=small_rows[:, FEATURES:], start=True, stop=True)
+        nc.scalar.copy(
             out=x_words[:].rearrange("p r j u q -> p (r j) u q")[:, :, :, 3 * QUADRANT :],
             in_=global_rows[:]
             .bitcast(F32)
@@ -158,6 +166,7 @@ def tile_edgemodel_pa_kernel(
             .unsqueeze(1)
             .to_broadcast([P, RING * CHUNK, 2, QUADRANT]),
         )
+        nc.scalar.copy(out=bias[:], in_=bias_spread[:])
 
         sort_chunk(0)
         for step in range(PAIRS + 3):

@@ -26,7 +26,6 @@ CHUNKS = TILES // CHUNK
 PAIRS_IN_CHUNK = CHUNK // PAIR
 RING = 2
 VECTOR_SORTS = 2
-LARGEST_F32 = 3.4028234663852886e38
 
 
 def tile_edgemodel_pa_kernel(
@@ -118,19 +117,10 @@ def tile_edgemodel_pa_kernel(
 
         def relu_and_store_pair(i):
             tiles = slice(i * PAIR, (i + 1) * PAIR)
-            if i % 4 == 3:
+            if i % 3 == 0:
                 nc.vector.tensor_scalar_max(out=result[:, tiles, :], in0=result[:, tiles, :], scalar1=0.0)
-            elif i % 4 != 1 or i >= PAIRS - 4:
-                nc.scalar.activation(out=result[:, tiles, :], in_=result[:, tiles, :], func=ACT.Relu)
             else:
-                nc.gpsimd.tensor_scalar(
-                    out=result[:, tiles, :],
-                    in0=result[:, tiles, :],
-                    scalar1=LARGEST_F32,
-                    scalar2=0.0,
-                    op0=ALU.min,
-                    op1=ALU.max,
-                )
+                nc.scalar.activation(out=result[:, tiles, :], in_=result[:, tiles, :], func=ACT.Relu)
             nc.sync.dma_start(out=out_rows[:, tiles, :], in_=result[:, tiles, :])
 
         nc.vector.memset(small_rows[:], 0.0)

@@ -25,7 +25,8 @@ CHUNK = 4
 CHUNKS = TILES // CHUNK
 PAIRS_IN_CHUNK = CHUNK // PAIR
 RING = 2
-VECTOR_SORTS = 2
+OWN = 3 * QUADRANT
+LARGEST_F32 = 3.4028234663852886e38
 
 
 def tile_edgemodel_pa_kernel(
@@ -47,15 +48,15 @@ def tile_edgemodel_pa_kernel(
         w_words = keep.tile([P, 2 * LATENT], U8, align_bytes=64)
         w_scales = keep.tile([P, LATENT], U8, align_bytes=64)
         ones = keep.tile([P, P], BF16)
-        small_rows = keep.tile([P, FEATURES + LATENT], BF16)
+        bias_row = keep.tile([P, LATENT], BF16)
         bias = keep.tile([P, LATENT], F32)
-        global_rows = keep.tile([P, FEATURES], BF16)
+        global_values = keep.tile([P, 4], BF16)
         table_warmer = keep.tile([P, 1], F32)
         loaded = [
             keep.tile([P, TILES, FEATURES], BF16, name="loaded_%d" % s) for s in range(len(streams))
         ]
         x_words = keep.tile([P, RING, CHUNK, 2, P], F32)
-        x_grouped = keep.tile([P, TILES, 4 * P], BF16, align_bytes=64)
+        x_grouped = keep.tile([P, RING, PAIR, 4 * P], BF16, align_bytes=64)
         x_codes = keep.tile([P, TILES, P], U32, align_bytes=64)
         x_scales = keep.tile([P, TILES, P], U8, align_bytes=64)
         result = keep.tile([P, TILES, LATENT], F32)
@@ -68,7 +69,7 @@ def tile_edgemodel_pa_kernel(
 
         def sort_chunk(c):
             tiles = slice(c * CHUNK, (c + 1) * CHUNK)
-            copy = nc.vector.tensor_copy if c < VECTOR_SORTS else nc.scalar.copy
+            copy = nc.vector.tensor_copy if c % 2 == 0 or c == 1 else nc.scalar.copy
             for s in range(len(streams)):
                 copy(
                     out=x_words[:, c % RING, :, :, s * QUADRANT : (s + 1) * QUADRANT],
@@ -76,7 +77,6 @@ def tile_edgemodel_pa_kernel(
                 )
 
         def transpose_pair(i):
-            tiles = slice(i * PAIR, (i + 1) * PAIR)
             planes = planes_pool.tile([P, PAIR, 2, P], F32)
             for jj in range(PAIR):
                 for u in range(2):
@@ -85,8 +85,8 @@ def tile_edgemodel_pa_kernel(
                         planes[:, jj, u, :], x_words[:, (j // CHUNK) % RING, j % CHUNK, u, :], identity[:]
                     )
             nc.scalar.copy(
-                out=x_grouped[:, tiles, :].bitcast(F32).rearrange("p j (e u) -> p j e u", u=2),
-                in_=planes[:].rearrange("p j u e -> p j e u"),
+                out=x_grouped[:OWN, i % RING, :, :].bitcast(F32).rearrange("p j (e u) -> p j e u", u=2),
+                in_=planes[:OWN].rearrange("p j u e -> p j e u"),
             )
 
         def quantise_pair(i):
@@ -94,7 +94,7 @@ def tile_edgemodel_pa_kernel(
             nc.vector.quantize_mx(
                 out=x_codes[:, tiles, :].rearrange("p j e -> p (j e)").bitcast(FP8X4),
                 scales=x_scales[:, tiles, :].rearrange("p j e -> p (j e)"),
-                in_=x_grouped[:, tiles, :].rearrange("p j c -> p (j c)"),
+                in_=x_grouped[:, i % RING, :, :].rearrange("p j c -> p (j c)"),
             )
 
         def multiply_pair(i):
@@ -117,15 +117,26 @@ def tile_edgemodel_pa_kernel(
 
         def relu_and_store_pair(i):
             tiles = slice(i * PAIR, (i + 1) * PAIR)
-            if i % 3 == 0:
+            if i == PAIRS - 1:
                 nc.vector.tensor_scalar_max(out=result[:, tiles, :], in0=result[:, tiles, :], scalar1=0.0)
-            else:
+            elif i % 2 == 0 or i >= PAIRS - 4:
                 nc.scalar.activation(out=result[:, tiles, :], in_=result[:, tiles, :], func=ACT.Relu)
+            else:
+                nc.gpsimd.tensor_scalar(
+                    out=result[:, tiles, :],
+                    in0=result[:, tiles, :],
+                    scalar1=LARGEST_F32,
+                    scalar2=0.0,
+                    op0=ALU.min,
+                    op1=ALU.max,
+                )
             nc.sync.dma_start(out=out_rows[:, tiles, :], in_=result[:, tiles, :])
 
-        nc.vector.memset(small_rows[:], 0.0)
-        nc.scalar.dma_start(out=small_rows[0:1, :FEATURES], in_=global_attr)
-        nc.scalar.dma_start(out=small_rows[0:1, FEATURES:], in_=b1.rearrange("(o n) -> o n", o=1))
+        nc.vector.memset(bias_row[:], 0.0)
+        nc.scalar.dma_start(
+            out=global_values[OWN:, :], in_=global_attr.rearrange("o (q t) -> (o q) t", t=4)
+        )
+        nc.scalar.dma_start(out=bias_row[0:1, :], in_=b1.rearrange("(o n) -> o n", o=1))
         load_chunk(0)
         nc.sync.dma_start(out=w_words[:].bitcast(I32), in_=W1_words[0].bitcast(I32))
         nc.vector.memset(w_scales[:].bitcast(I32), 0)
@@ -138,27 +149,19 @@ def tile_edgemodel_pa_kernel(
             load_chunk(c)
 
         make_identity(nc, identity[:])
+        nc.gpsimd.memset(x_words[:].rearrange("p r j u q -> p (r j) u q")[:, :, :, OWN:], 0.0)
         nc.vector.memset(table_warmer[:], 0.0)
         nc.scalar.activation(out=table_warmer[:], in_=table_warmer[:], func=ACT.Relu)
-        nc.vector.memset(ones[:], 1.0)
-        global_spread = sums_pool.tile([P, LATENT], F32, name="acc")
-        nc.tensor.matmul(
-            out=global_spread[:, :FEATURES], lhsT=ones[:], rhs=small_rows[:, :FEATURES], start=True, stop=True
-        )
-        nc.scalar.copy(out=global_rows[:], in_=global_spread[:, :FEATURES])
-        bias_spread = sums_pool.tile([P, LATENT], F32, name="acc")
-        nc.tensor.matmul(out=bias_spread[:], lhsT=ones[:], rhs=small_rows[:, FEATURES:], start=True, stop=True)
         nc.scalar.copy(
-            out=x_words[:].rearrange("p r j u q -> p (r j) u q")[:, :, :, 3 * QUADRANT :],
-            in_=global_rows[:]
-            .bitcast(F32)
-            .rearrange("p (q u) -> p u q", u=2)
-            .unsqueeze(1)
-            .to_broadcast([P, RING * CHUNK, 2, QUADRANT]),
+            out=x_grouped[OWN:].bitcast(F32).rearrange("p r j (e u) -> p (r j e) u", u=2),
+            in_=global_values[OWN:, :].bitcast(F32).unsqueeze(1).to_broadcast([QUADRANT, RING * PAIR * P, 2]),
         )
-        nc.scalar.copy(out=bias[:], in_=bias_spread[:])
+        nc.vector.memset(ones[:], 1.0)
+        bias_spread = sums_pool.tile([P, LATENT], F32, name="acc")
+        nc.tensor.matmul(out=bias_spread[:], lhsT=ones[:], rhs=bias_row[:], start=True, stop=True)
 
         sort_chunk(0)
+        nc.vector.tensor_copy(out=bias[:], in_=bias_spread[:])
         for step in range(PAIRS + 3):
             if step < PAIRS:
                 transpose_pair(step)

@@ -20,13 +20,12 @@ FEATURES = 128
 QUADRANT = FEATURES // 4
 LATENT = 512
 PAIR = 2
-PAIRS = TILES // PAIR
-CHUNK = 4
-CHUNKS = TILES // CHUNK
-PAIRS_IN_CHUNK = CHUNK // PAIR
-RING = 2
+SLOTS = 4
 OWN = 3 * QUADRANT
 LARGEST_F32 = 3.4028234663852886e38
+GROUP_SIZES = (2, 2, 4, 4, 4, 4, 4, 4, 2, 2)
+LOADS = ((0, 4), (4, 8), (8, 12), (12, 16), (16, 24), (24, 32))
+VECTOR_SORTS = 12
 
 
 def tile_edgemodel_pa_kernel(
@@ -37,6 +36,12 @@ def tile_edgemodel_pa_kernel(
         piece.rearrange("(p j) k -> p j k", j=TILES) for piece in (receiver, sender, edge_attr)
     ]
     out_rows = out.rearrange("(p j) n -> p j n", j=TILES)
+    groups = []
+    first = 0
+    for size in GROUP_SIZES:
+        groups.append((first, first + size))
+        first += size
+    count = len(groups)
 
     with (
         tc.tile_pool(name="keep", bufs=1) as keep,
@@ -55,89 +60,89 @@ def tile_edgemodel_pa_kernel(
         loaded = [
             keep.tile([P, TILES, FEATURES], BF16, name="loaded_%d" % s) for s in range(len(streams))
         ]
-        x_words = keep.tile([P, RING, CHUNK, 2, P], F32)
-        x_grouped = keep.tile([P, RING, PAIR, 4 * P], BF16, align_bytes=64)
+        x_words = keep.tile([P, TILES, 2, P], F32)
+        x_grouped = keep.tile([P, SLOTS, PAIR, 4 * P], BF16, align_bytes=64)
         x_codes = keep.tile([P, TILES, P], U32, align_bytes=64)
         x_scales = keep.tile([P, TILES, P], U8, align_bytes=64)
         result = keep.tile([P, TILES, LATENT], F32)
         sums = {}
 
-        def load_chunk(c):
-            tiles = slice(c * CHUNK, (c + 1) * CHUNK)
+        def load(lo, hi):
             for s, stream in enumerate(streams):
-                nc.sync.dma_start(out=loaded[s][:, tiles, :], in_=stream[:, tiles, :])
+                nc.sync.dma_start(out=loaded[s][:, lo:hi, :], in_=stream[:, lo:hi, :])
 
-        def sort_chunk(c):
-            tiles = slice(c * CHUNK, (c + 1) * CHUNK)
-            copy = nc.vector.tensor_copy if c % 2 == 0 or c == 1 else nc.scalar.copy
+        def sort(lo, hi, copy):
             for s in range(len(streams)):
                 copy(
-                    out=x_words[:, c % RING, :, :, s * QUADRANT : (s + 1) * QUADRANT],
-                    in_=loaded[s][:, tiles, :].bitcast(F32).rearrange("p j (q u) -> p j u q", u=2),
+                    out=x_words[:, lo:hi, :, s * QUADRANT : (s + 1) * QUADRANT],
+                    in_=loaded[s][:, lo:hi, :].bitcast(F32).rearrange("p j (q u) -> p j u q", u=2),
                 )
+
+        def prefill(slot):
+            nc.scalar.copy(
+                out=x_grouped[OWN:, slot].bitcast(F32).rearrange("p j (e u) -> p (j e) u", u=2),
+                in_=global_values[OWN:, :].bitcast(F32).unsqueeze(1).to_broadcast([QUADRANT, PAIR * P, 2]),
+            )
 
         def transpose_pair(i):
             planes = planes_pool.tile([P, PAIR, 2, P], F32)
             for jj in range(PAIR):
                 for u in range(2):
-                    j = i * PAIR + jj
-                    nc.tensor.transpose(
-                        planes[:, jj, u, :], x_words[:, (j // CHUNK) % RING, j % CHUNK, u, :], identity[:]
-                    )
+                    nc.tensor.transpose(planes[:, jj, u, :], x_words[:, i * PAIR + jj, u, :], identity[:])
             nc.scalar.copy(
-                out=x_grouped[:OWN, i % RING, :, :].bitcast(F32).rearrange("p j (e u) -> p j e u", u=2),
+                out=x_grouped[:OWN, i % SLOTS, :, :].bitcast(F32).rearrange("p j (e u) -> p j e u", u=2),
                 in_=planes[:OWN].rearrange("p j u e -> p j e u"),
             )
 
-        def quantise_pair(i):
-            tiles = slice(i * PAIR, (i + 1) * PAIR)
+        def quantise(lo, hi):
+            slot = (lo // PAIR) % SLOTS
             nc.vector.quantize_mx(
-                out=x_codes[:, tiles, :].rearrange("p j e -> p (j e)").bitcast(FP8X4),
-                scales=x_scales[:, tiles, :].rearrange("p j e -> p (j e)"),
-                in_=x_grouped[:, i % RING, :, :].rearrange("p j c -> p (j c)"),
+                out=x_codes[:, lo:hi, :].rearrange("p j e -> p (j e)").bitcast(FP8X4),
+                scales=x_scales[:, lo:hi, :].rearrange("p j e -> p (j e)"),
+                in_=x_grouped[:, slot : slot + (hi - lo) // PAIR, :, :].rearrange("p r j c -> p (r j c)"),
             )
 
-        def multiply_pair(i):
-            for j in range(i * PAIR, (i + 1) * PAIR):
-                acc = sums_pool.tile([P, LATENT], F32)
-                nc.tensor.matmul_mx(
-                    out=acc[:],
-                    lhsT=x_codes[:, j, :].bitcast(FP8X4),
-                    lhsT_scale=x_scales[:, j, :],
-                    rhs=w_words[:].bitcast(FP4X4),
-                    rhs_scale=w_scales[:],
-                    start=True,
-                    stop=True,
-                )
-                sums[j] = acc
+        def multiply(j):
+            acc = sums_pool.tile([P, LATENT], F32)
+            nc.tensor.matmul_mx(
+                out=acc[:],
+                lhsT=x_codes[:, j, :].bitcast(FP8X4),
+                lhsT_scale=x_scales[:, j, :],
+                rhs=w_words[:].bitcast(FP4X4),
+                rhs_scale=w_scales[:],
+                start=True,
+                stop=True,
+            )
+            sums[j] = acc
 
-        def add_bias_pair(i):
-            for j in range(i * PAIR, (i + 1) * PAIR):
-                nc.vector.tensor_tensor(out=result[:, j, :], in0=sums[j][:], in1=bias[:], op=ALU.add)
+        def add_bias(j):
+            nc.vector.tensor_tensor(out=result[:, j, :], in0=sums[j][:], in1=bias[:], op=ALU.add)
 
-        def relu_and_store_pair(i):
-            tiles = slice(i * PAIR, (i + 1) * PAIR)
-            if i == PAIRS - 1:
-                nc.vector.tensor_scalar_max(out=result[:, tiles, :], in0=result[:, tiles, :], scalar1=0.0)
-            elif i % 2 == 0 or i >= PAIRS - 4:
-                nc.scalar.activation(out=result[:, tiles, :], in_=result[:, tiles, :], func=ACT.Relu)
-            else:
-                nc.gpsimd.tensor_scalar(
-                    out=result[:, tiles, :],
-                    in0=result[:, tiles, :],
-                    scalar1=LARGEST_F32,
-                    scalar2=0.0,
-                    op0=ALU.min,
-                    op1=ALU.max,
-                )
-            nc.sync.dma_start(out=out_rows[:, tiles, :], in_=result[:, tiles, :])
+        def relu_gpsimd(lo, hi):
+            nc.gpsimd.tensor_scalar(
+                out=result[:, lo:hi, :],
+                in0=result[:, lo:hi, :],
+                scalar1=LARGEST_F32,
+                scalar2=0.0,
+                op0=ALU.min,
+                op1=ALU.max,
+            )
+
+        def relu_scalar(lo, hi):
+            nc.scalar.activation(out=result[:, lo:hi, :], in_=result[:, lo:hi, :], func=ACT.Relu)
+
+        def relu_vector(lo, hi):
+            nc.vector.tensor_scalar_max(out=result[:, lo:hi, :], in0=result[:, lo:hi, :], scalar1=0.0)
+
+        def store(lo, hi):
+            nc.sync.dma_start(out=out_rows[:, lo:hi, :], in_=result[:, lo:hi, :])
 
         nc.vector.memset(bias_row[:], 0.0)
         nc.scalar.dma_start(
             out=global_values[OWN:, :], in_=global_attr.rearrange("o (q t) -> (o q) t", t=4)
         )
         nc.scalar.dma_start(out=bias_row[0:1, :], in_=b1.rearrange("(o n) -> o n", o=1))
-        load_chunk(0)
+        load(*LOADS[0])
         nc.sync.dma_start(out=w_words[:].bitcast(I32), in_=W1_words[0].bitcast(I32))
         nc.vector.memset(w_scales[:].bitcast(I32), 0)
         for quadrant in range(4):
@@ -145,32 +150,64 @@ def tile_edgemodel_pa_kernel(
                 out=w_scales[32 * quadrant : 32 * quadrant + 4, :].bitcast(I32),
                 in_=W1_scales[0, 4 * quadrant : 4 * quadrant + 4, :].bitcast(I32),
             )
-        for c in range(1, CHUNKS):
-            load_chunk(c)
+        for lo, hi in LOADS[1:]:
+            load(lo, hi)
 
         make_identity(nc, identity[:])
-        nc.gpsimd.memset(x_words[:].rearrange("p r j u q -> p (r j) u q")[:, :, :, OWN:], 0.0)
+        nc.gpsimd.memset(x_words[:].rearrange("p j u q -> p (j u) q")[:, :, OWN:], 0.0)
         nc.vector.memset(table_warmer[:], 0.0)
         nc.scalar.activation(out=table_warmer[:], in_=table_warmer[:], func=ACT.Relu)
-        nc.scalar.copy(
-            out=x_grouped[OWN:].bitcast(F32).rearrange("p r j (e u) -> p (r j e) u", u=2),
-            in_=global_values[OWN:, :].bitcast(F32).unsqueeze(1).to_broadcast([QUADRANT, RING * PAIR * P, 2]),
-        )
         nc.vector.memset(ones[:], 1.0)
-        bias_spread = sums_pool.tile([P, LATENT], F32, name="acc")
-        nc.tensor.matmul(out=bias_spread[:], lhsT=ones[:], rhs=bias_row[:], start=True, stop=True)
+        prefill(0)
+        prefill(1)
 
-        sort_chunk(0)
-        nc.vector.tensor_copy(out=bias[:], in_=bias_spread[:])
-        for step in range(PAIRS + 3):
-            if step < PAIRS:
-                transpose_pair(step)
-                if step % PAIRS_IN_CHUNK == 0 and step // PAIRS_IN_CHUNK + 1 < CHUNKS:
-                    sort_chunk(step // PAIRS_IN_CHUNK + 1)
-            if 0 <= step - 1 < PAIRS:
-                quantise_pair(step - 1)
-                multiply_pair(step - 1)
-            if 0 <= step - 2 < PAIRS:
-                add_bias_pair(step - 2)
-            if 0 <= step - 3 < PAIRS:
-                relu_and_store_pair(step - 3)
+        sort(0, 2, nc.vector.tensor_copy)
+        sort(2, 4, nc.vector.tensor_copy)
+        for step in range(count + 4):
+            if step < count:
+                for i in range(groups[step][0] // PAIR, groups[step][1] // PAIR):
+                    transpose_pair(i)
+            if step == 0:
+                sort(4, 8, nc.vector.tensor_copy)
+            if step == 1:
+                prefill(2)
+                prefill(3)
+                bias_spread = sums_pool.tile([P, LATENT], F32, name="acc")
+                nc.tensor.matmul(out=bias_spread[:], lhsT=ones[:], rhs=bias_row[:], start=True, stop=True)
+            if step + 2 < count and groups[step + 2][0] >= VECTOR_SORTS:
+                sort(groups[step + 2][0], groups[step + 2][1], nc.scalar.copy)
+            if 0 <= step - 3 < count - 1:
+                lo, hi = groups[step - 3]
+                half = (lo + hi) // 2
+                relu_scalar(half, hi)
+                store(half, hi)
+            made = []
+            if 0 <= step - 1 < count:
+                lo, hi = groups[step - 1]
+                quantise(lo, hi)
+                made = list(range(lo, hi))
+            if step == 1:
+                nc.vector.tensor_copy(out=bias[:], in_=bias_spread[:])
+                sort(8, 12, nc.vector.tensor_copy)
+            for j in made[:2]:
+                multiply(j)
+            if 0 <= step - 2 < count:
+                lo, hi = groups[step - 2]
+                half = (lo + hi) // 2
+                for n, j in enumerate(range(lo, hi)):
+                    add_bias(j)
+                    if n + 2 < len(made):
+                        multiply(made[n + 2])
+                    if step - 2 == count - 1:
+                        if j < half:
+                            relu_scalar(j, j + 1)
+                        else:
+                            relu_vector(j, j + 1)
+                        store(j, j + 1)
+                    elif j < half:
+                        relu_gpsimd(j, j + 1)
+                        if j == half - 1:
+                            store(lo, half)
+            else:
+                for j in made[2:]:
+                    multiply(j)

@@ -25,7 +25,7 @@ OWN = 3 * QUADRANT
 LARGEST_F32 = 3.4028234663852886e38
 GROUP_SIZES = (2, 2, 4, 4, 4, 4, 4, 4, 2, 2)
 LOADS = ((0, 4), (4, 8), (8, 12), (12, 16), (16, 24), (24, 32))
-VECTOR_SORTS = 12
+VECTOR_SORTS = 8
 
 
 def tile_edgemodel_pa_kernel(
@@ -82,6 +82,16 @@ def tile_edgemodel_pa_kernel(
             nc.scalar.copy(
                 out=x_grouped[OWN:, slot].bitcast(F32).rearrange("p j (e u) -> p (j e) u", u=2),
                 in_=global_values[OWN:, :].bitcast(F32).unsqueeze(1).to_broadcast([QUADRANT, PAIR * P, 2]),
+            )
+
+        def prefill_gpsimd(slot):
+            nc.gpsimd.tensor_scalar(
+                out=x_grouped[OWN:, slot].rearrange("p j (e t) -> p (j e) t", t=4),
+                in0=global_values[OWN:, :].unsqueeze(1).to_broadcast([QUADRANT, PAIR * P, 4]),
+                scalar1=LARGEST_F32,
+                scalar2=-LARGEST_F32,
+                op0=ALU.min,
+                op1=ALU.max,
             )
 
         def transpose_pair(i):
@@ -154,14 +164,21 @@ def tile_edgemodel_pa_kernel(
             load(lo, hi)
 
         make_identity(nc, identity[:])
-        nc.gpsimd.memset(x_words[:].rearrange("p j u q -> p (j u) q")[:, :, OWN:], 0.0)
+        unused = x_words[:].rearrange("p j u q -> p (j u) q")[:, :, OWN:]
+        nc.vector.memset(unused[:, :TILES, :], 0.0)
+        nc.gpsimd.memset(unused[:, TILES:, :], 0.0)
         nc.vector.memset(table_warmer[:], 0.0)
         nc.scalar.activation(out=table_warmer[:], in_=table_warmer[:], func=ACT.Relu)
         nc.vector.memset(ones[:], 1.0)
         prefill(0)
         prefill(1)
+        prefill_gpsimd(2)
+        prefill_gpsimd(3)
 
+        bias_spread = sums_pool.tile([P, LATENT], F32, name="acc")
+        nc.tensor.matmul(out=bias_spread[:], lhsT=ones[:], rhs=bias_row[:], start=True, stop=True)
         sort(0, 2, nc.vector.tensor_copy)
+        nc.vector.tensor_copy(out=bias[:], in_=bias_spread[:])
         sort(2, 4, nc.vector.tensor_copy)
         for step in range(count + 4):
             if step < count:
@@ -169,26 +186,18 @@ def tile_edgemodel_pa_kernel(
                     transpose_pair(i)
             if step == 0:
                 sort(4, 8, nc.vector.tensor_copy)
-            if step == 1:
-                prefill(2)
-                prefill(3)
-                bias_spread = sums_pool.tile([P, LATENT], F32, name="acc")
-                nc.tensor.matmul(out=bias_spread[:], lhsT=ones[:], rhs=bias_row[:], start=True, stop=True)
             if step + 2 < count and groups[step + 2][0] >= VECTOR_SORTS:
                 sort(groups[step + 2][0], groups[step + 2][1], nc.scalar.copy)
             if 0 <= step - 3 < count - 1:
                 lo, hi = groups[step - 3]
                 half = (lo + hi) // 2
-                relu_scalar(half, hi)
+                relu_scalar(hi - 1, hi)
                 store(half, hi)
             made = []
             if 0 <= step - 1 < count:
                 lo, hi = groups[step - 1]
                 quantise(lo, hi)
                 made = list(range(lo, hi))
-            if step == 1:
-                nc.vector.tensor_copy(out=bias[:], in_=bias_spread[:])
-                sort(8, 12, nc.vector.tensor_copy)
             for j in made[:2]:
                 multiply(j)
             if 0 <= step - 2 < count:
@@ -204,7 +213,7 @@ def tile_edgemodel_pa_kernel(
                         else:
                             relu_vector(j, j + 1)
                         store(j, j + 1)
-                    elif j < half:
+                    elif j < hi - 1:
                         relu_gpsimd(j, j + 1)
                         if j == half - 1:
                             store(lo, half)

@@ -153,6 +153,7 @@ def tile_edgemodel_pa_kernel(
         )
         nc.scalar.dma_start(out=bias_row[0:1, :], in_=b1.rearrange("(o n) -> o n", o=1))
         load(*LOADS[0])
+        load(*LOADS[1])
         nc.sync.dma_start(out=w_words[:].bitcast(I32), in_=W1_words[0].bitcast(I32))
         nc.vector.memset(w_scales[:].bitcast(I32), 0)
         for quadrant in range(4):
@@ -160,7 +161,7 @@ def tile_edgemodel_pa_kernel(
                 out=w_scales[32 * quadrant : 32 * quadrant + 4, :].bitcast(I32),
                 in_=W1_scales[0, 4 * quadrant : 4 * quadrant + 4, :].bitcast(I32),
             )
-        for lo, hi in LOADS[1:]:
+        for lo, hi in LOADS[2:]:
             load(lo, hi)
 
         make_identity(nc, identity[:])
@@ -175,10 +176,7 @@ def tile_edgemodel_pa_kernel(
         prefill_gpsimd(2)
         prefill_gpsimd(3)
 
-        bias_spread = sums_pool.tile([P, LATENT], F32, name="acc")
-        nc.tensor.matmul(out=bias_spread[:], lhsT=ones[:], rhs=bias_row[:], start=True, stop=True)
         sort(0, 2, nc.vector.tensor_copy)
-        nc.vector.tensor_copy(out=bias[:], in_=bias_spread[:])
         sort(2, 4, nc.vector.tensor_copy)
         for step in range(count + 4):
             if step < count:
@@ -186,6 +184,9 @@ def tile_edgemodel_pa_kernel(
                     transpose_pair(i)
             if step == 0:
                 sort(4, 8, nc.vector.tensor_copy)
+            if step == 1:
+                bias_spread = sums_pool.tile([P, LATENT], F32, name="acc")
+                nc.tensor.matmul(out=bias_spread[:], lhsT=ones[:], rhs=bias_row[:], start=True, stop=True)
             if step + 2 < count and groups[step + 2][0] >= VECTOR_SORTS:
                 sort(groups[step + 2][0], groups[step + 2][1], nc.scalar.copy)
             if 0 <= step - 3 < count - 1:
@@ -198,6 +199,8 @@ def tile_edgemodel_pa_kernel(
                 lo, hi = groups[step - 1]
                 quantise(lo, hi)
                 made = list(range(lo, hi))
+            if step == 1:
+                nc.vector.tensor_copy(out=bias[:], in_=bias_spread[:])
             for j in made[:2]:
                 multiply(j)
             if 0 <= step - 2 < count:

@@ -25,6 +25,7 @@ OWN = 3 * QUADRANT
 LARGEST_F32 = 3.4028234663852886e38
 GROUP_SIZES = (2, 2, 4, 4, 4, 4, 4, 4, 2, 2)
 LOADS = ((0, 4), (4, 8), (8, 12), (12, 16), (16, 24), (24, 32))
+GPSIMD_PART = 320
 VECTOR_SORTS = 8
 
 
@@ -192,7 +193,11 @@ def tile_edgemodel_pa_kernel(
             if 0 <= step - 3 < count - 1:
                 lo, hi = groups[step - 3]
                 half = (lo + hi) // 2
-                relu_scalar(hi - 1, hi)
+                if hi - lo == 4:
+                    tail_of_pair = result[:, hi - 2 : hi, :].rearrange("p j n -> p (j n)")[:, GPSIMD_PART:]
+                    nc.scalar.activation(out=tail_of_pair, in_=tail_of_pair, func=ACT.Relu)
+                else:
+                    relu_scalar(hi - 1, hi)
                 store(half, hi)
             made = []
             if 0 <= step - 1 < count:
@@ -216,6 +221,15 @@ def tile_edgemodel_pa_kernel(
                         else:
                             relu_vector(j, j + 1)
                         store(j, j + 1)
+                    elif j == hi - 2 and hi - lo == 4:
+                        nc.gpsimd.tensor_scalar(
+                            out=result[:, j, :GPSIMD_PART],
+                            in0=result[:, j, :GPSIMD_PART],
+                            scalar1=LARGEST_F32,
+                            scalar2=0.0,
+                            op0=ALU.min,
+                            op1=ALU.max,
+                        )
                     elif j < hi - 1:
                         relu_gpsimd(j, j + 1)
                         if j == half - 1:

@@ -61,7 +61,7 @@ def tile_edgemodel_pa_kernel(
         loaded = [
             keep.tile([P, TILES, FEATURES], BF16, name="loaded_%d" % s) for s in range(len(streams))
         ]
-        x_words = keep.tile([P, TILES, 2, P], F32)
+        x_words = keep.tile([P, TILES, 2 * OWN + QUADRANT], F32)
         x_grouped = keep.tile([P, SLOTS, PAIR, 4 * P], BF16, align_bytes=64)
         x_codes = keep.tile([P, TILES, P], U32, align_bytes=64)
         x_scales = keep.tile([P, TILES, P], U8, align_bytes=64)
@@ -75,31 +75,23 @@ def tile_edgemodel_pa_kernel(
         def sort(lo, hi, copy):
             for s in range(len(streams)):
                 copy(
-                    out=x_words[:, lo:hi, :, s * QUADRANT : (s + 1) * QUADRANT],
+                    out=x_words[:, lo:hi, : 2 * OWN].rearrange("p j (u q) -> p j u q", u=2)[
+                        :, :, :, s * QUADRANT : (s + 1) * QUADRANT
+                    ],
                     in_=loaded[s][:, lo:hi, :].bitcast(F32).rearrange("p j (q u) -> p j u q", u=2),
                 )
 
-        def prefill(slot):
-            nc.scalar.copy(
+        def prefill(slot, copy):
+            copy(
                 out=x_grouped[OWN:, slot].bitcast(F32).rearrange("p j (e u) -> p (j e) u", u=2),
                 in_=global_values[OWN:, :].bitcast(F32).unsqueeze(1).to_broadcast([QUADRANT, PAIR * P, 2]),
-            )
-
-        def prefill_gpsimd(slot):
-            nc.gpsimd.tensor_scalar(
-                out=x_grouped[OWN:, slot].rearrange("p j (e t) -> p (j e) t", t=4),
-                in0=global_values[OWN:, :].unsqueeze(1).to_broadcast([QUADRANT, PAIR * P, 4]),
-                scalar1=LARGEST_F32,
-                scalar2=-LARGEST_F32,
-                op0=ALU.min,
-                op1=ALU.max,
             )
 
         def transpose_pair(i):
             planes = planes_pool.tile([P, PAIR, 2, P], F32)
             for jj in range(PAIR):
                 for u in range(2):
-                    nc.tensor.transpose(planes[:, jj, u, :], x_words[:, i * PAIR + jj, u, :], identity[:])
+                    nc.tensor.transpose(planes[:, jj, u, :], x_words[:, i * PAIR + jj, u * OWN : u * OWN + P], identity[:])
             nc.scalar.copy(
                 out=x_grouped[:OWN, i % SLOTS, :, :].bitcast(F32).rearrange("p j (e u) -> p j e u", u=2),
                 in_=planes[:OWN].rearrange("p j u e -> p j e u"),
@@ -166,16 +158,14 @@ def tile_edgemodel_pa_kernel(
             load(lo, hi)
 
         make_identity(nc, identity[:])
-        unused = x_words[:].rearrange("p j u q -> p (j u) q")[:, :, OWN:]
-        nc.vector.memset(unused[:, :TILES, :], 0.0)
-        nc.gpsimd.memset(unused[:, TILES:, :], 0.0)
         nc.vector.memset(table_warmer[:], 0.0)
         nc.scalar.activation(out=table_warmer[:], in_=table_warmer[:], func=ACT.Relu)
         nc.vector.memset(ones[:], 1.0)
-        prefill(0)
-        prefill(1)
-        prefill_gpsimd(2)
-        prefill_gpsimd(3)
+        nc.vector.memset(x_words[:, :, 2 * OWN :], 0.0)
+        prefill(0, nc.vector.tensor_copy)
+        prefill(1, nc.vector.tensor_copy)
+        prefill(2, nc.scalar.copy)
+        prefill(3, nc.scalar.copy)
 
         sort(0, 2, nc.vector.tensor_copy)
         sort(2, 4, nc.vector.tensor_copy)

@@ -25,7 +25,7 @@ OWN = 3 * QUADRANT
 LARGEST_F32 = 3.4028234663852886e38
 GROUP_SIZES = (2, 2, 4, 4, 4, 4, 4, 4, 2, 2)
 LOADS = ((0, 4), (4, 8), (8, 12), (12, 16), (16, 24), (24, 32))
-GPSIMD_PART = 320
+SCALAR_PART = 192
 VECTOR_SORTS = 8
 
 
@@ -184,8 +184,8 @@ def tile_edgemodel_pa_kernel(
                 lo, hi = groups[step - 3]
                 half = (lo + hi) // 2
                 if hi - lo == 4:
-                    tail_of_pair = result[:, hi - 2 : hi, :].rearrange("p j n -> p (j n)")[:, GPSIMD_PART:]
-                    nc.scalar.activation(out=tail_of_pair, in_=tail_of_pair, func=ACT.Relu)
+                    head_of_pair = result[:, hi - 2 : hi, :].rearrange("p j n -> p (j n)")[:, : LATENT + SCALAR_PART]
+                    nc.scalar.activation(out=head_of_pair, in_=head_of_pair, func=ACT.Relu)
                 else:
                     relu_scalar(hi - 1, hi)
                 store(half, hi)
@@ -211,16 +211,16 @@ def tile_edgemodel_pa_kernel(
                         else:
                             relu_vector(j, j + 1)
                         store(j, j + 1)
-                    elif j == hi - 2 and hi - lo == 4:
+                    elif j == hi - 1 and hi - lo == 4:
                         nc.gpsimd.tensor_scalar(
-                            out=result[:, j, :GPSIMD_PART],
-                            in0=result[:, j, :GPSIMD_PART],
+                            out=result[:, j, SCALAR_PART:],
+                            in0=result[:, j, SCALAR_PART:],
                             scalar1=LARGEST_F32,
                             scalar2=0.0,
                             op0=ALU.min,
                             op1=ALU.max,
                         )
-                    elif j < hi - 1:
+                    elif j < half:
                         relu_gpsimd(j, j + 1)
                         if j == half - 1:
                             store(lo, half)

@@ -25,7 +25,8 @@ OWN = 3 * QUADRANT
 LARGEST_F32 = 3.4028234663852886e38
 GROUP_SIZES = (2, 2, 4, 4, 4, 4, 4, 4, 2, 2)
 LOADS = ((0, 4), (4, 8), (8, 12), (12, 16), (16, 24), (24, 32))
-SCALAR_PART = 192
+SCALAR_RELUS = {2: (1,), 4: (2,)}
+LATE = 6
 VECTOR_SORTS = 8
 
 
@@ -169,26 +170,18 @@ def tile_edgemodel_pa_kernel(
 
         sort(0, 2, nc.vector.tensor_copy)
         sort(2, 4, nc.vector.tensor_copy)
+        bias_spread = sums_pool.tile([P, LATENT], F32, name="acc")
         for step in range(count + 4):
-            if step < count:
-                for i in range(groups[step][0] // PAIR, groups[step][1] // PAIR):
-                    transpose_pair(i)
+            for g in {1: (1, 2), 2: ()}.get(step, (step,)):
+                if g == 2:
+                    nc.tensor.matmul(out=bias_spread[:], lhsT=ones[:], rhs=bias_row[:], start=True, stop=True)
+                if g < count:
+                    for i in range(groups[g][0] // PAIR, groups[g][1] // PAIR):
+                        transpose_pair(i)
             if step == 0:
                 sort(4, 8, nc.vector.tensor_copy)
-            if step == 1:
-                bias_spread = sums_pool.tile([P, LATENT], F32, name="acc")
-                nc.tensor.matmul(out=bias_spread[:], lhsT=ones[:], rhs=bias_row[:], start=True, stop=True)
             if step + 2 < count and groups[step + 2][0] >= VECTOR_SORTS:
                 sort(groups[step + 2][0], groups[step + 2][1], nc.scalar.copy)
-            if 0 <= step - 3 < count - 1:
-                lo, hi = groups[step - 3]
-                half = (lo + hi) // 2
-                if hi - lo == 4:
-                    head_of_pair = result[:, hi - 2 : hi, :].rearrange("p j n -> p (j n)")[:, : LATENT + SCALAR_PART]
-                    nc.scalar.activation(out=head_of_pair, in_=head_of_pair, func=ACT.Relu)
-                else:
-                    relu_scalar(hi - 1, hi)
-                store(half, hi)
             made = []
             if 0 <= step - 1 < count:
                 lo, hi = groups[step - 1]
@@ -205,25 +198,16 @@ def tile_edgemodel_pa_kernel(
                     add_bias(j)
                     if n + 2 < len(made):
                         multiply(made[n + 2])
-                    if step - 2 == count - 1:
-                        if j < half:
-                            relu_scalar(j, j + 1)
-                        else:
-                            relu_vector(j, j + 1)
-                        store(j, j + 1)
-                    elif j == hi - 1 and hi - lo == 4:
-                        nc.gpsimd.tensor_scalar(
-                            out=result[:, j, SCALAR_PART:],
-                            in0=result[:, j, SCALAR_PART:],
-                            scalar1=LARGEST_F32,
-                            scalar2=0.0,
-                            op0=ALU.min,
-                            op1=ALU.max,
-                        )
-                    elif j < half:
+                    if step - 2 == count - 1 and j >= half:
+                        relu_vector(j, j + 1)
+                    elif (step - 2 >= 2 and n in SCALAR_RELUS[hi - lo]) or (step - 2 >= LATE and j >= half) or step - 2 == count - 1:
+                        relu_scalar(j, j + 1)
+                    else:
                         relu_gpsimd(j, j + 1)
-                        if j == half - 1:
-                            store(lo, half)
+                    if hi - lo == 2:
+                        store(j, j + 1)
+                    elif n % 2 == 1:
+                        store(j - 1, j + 1)
             else:
                 for j in made[2:]:
                     multiply(j)

@@ -25,8 +25,8 @@ OWN = 3 * QUADRANT
 LARGEST_F32 = 3.4028234663852886e38
 GROUP_SIZES = (2, 2, 4, 4, 4, 4, 4, 4, 2, 2)
 LOADS = ((0, 4), (4, 8), (8, 12), (12, 16), (16, 24), (24, 32))
-SCALAR_RELUS = {2: (1,), 4: (2,)}
-LATE = 6
+LATE = 5
+
 VECTOR_SORTS = 8
 
 
@@ -73,8 +73,8 @@ def tile_edgemodel_pa_kernel(
             for s, stream in enumerate(streams):
                 nc.sync.dma_start(out=loaded[s][:, lo:hi, :], in_=stream[:, lo:hi, :])
 
-        def sort(lo, hi, copy):
-            for s in range(len(streams)):
+        def sort(lo, hi, copy, pieces=range(3)):
+            for s in pieces:
                 copy(
                     out=x_words[:, lo:hi, : 2 * OWN].rearrange("p j (u q) -> p j u q", u=2)[
                         :, :, :, s * QUADRANT : (s + 1) * QUADRANT
@@ -88,8 +88,8 @@ def tile_edgemodel_pa_kernel(
                 in_=global_values[OWN:, :].bitcast(F32).unsqueeze(1).to_broadcast([QUADRANT, PAIR * P, 2]),
             )
 
-        def transpose_pair(i):
-            planes = planes_pool.tile([P, PAIR, 2, P], F32)
+        def transpose_pair(i, pool, name):
+            planes = pool.tile([P, PAIR, 2, P], F32, name=name)
             for jj in range(PAIR):
                 for u in range(2):
                     nc.tensor.transpose(planes[:, jj, u, :], x_words[:, i * PAIR + jj, u * OWN : u * OWN + P], identity[:])
@@ -138,6 +138,11 @@ def tile_edgemodel_pa_kernel(
         def relu_vector(lo, hi):
             nc.vector.tensor_scalar_max(out=result[:, lo:hi, :], in0=result[:, lo:hi, :], scalar1=0.0)
 
+        def relu(group, n, j):
+            size = groups[group][1] - groups[group][0]
+            pat = "GG" if group < 2 else "SV" if group == count - 1 else "GS" if size == 2 else "GGSS" if group >= 6 else "GGSG"
+            {"G": relu_gpsimd, "S": relu_scalar, "V": relu_vector}[pat[n]](j, j + 1)
+
         def store(lo, hi):
             nc.sync.dma_start(out=out_rows[:, lo:hi, :], in_=result[:, lo:hi, :])
 
@@ -168,46 +173,59 @@ def tile_edgemodel_pa_kernel(
         prefill(2, nc.scalar.copy)
         prefill(3, nc.scalar.copy)
 
+        def front(group, pool=planes_pool, name="planes"):
+            for i in range(groups[group][0] // PAIR, groups[group][1] // PAIR):
+                transpose_pair(i, pool, name)
+
+        def finish(group, n):
+            j = groups[group][0] + n
+            add_bias(j)
+            relu(group, n, j)
+            k = [2,2,2,2,2,2,2,2,2,2][group]
+            if (n + 1) % k == 0:
+                store(j + 1 - k, j + 1)
+
         sort(0, 2, nc.vector.tensor_copy)
         sort(2, 4, nc.vector.tensor_copy)
+        front(0)
+        sort(4, 8, nc.vector.tensor_copy)
+        front(1)
         bias_spread = sums_pool.tile([P, LATENT], F32, name="acc")
-        for step in range(count + 4):
-            for g in {1: (1, 2), 2: ()}.get(step, (step,)):
-                if g == 2:
-                    nc.tensor.matmul(out=bias_spread[:], lhsT=ones[:], rhs=bias_row[:], start=True, stop=True)
-                if g < count:
-                    for i in range(groups[g][0] // PAIR, groups[g][1] // PAIR):
-                        transpose_pair(i)
-            if step == 0:
-                sort(4, 8, nc.vector.tensor_copy)
-            if step + 2 < count and groups[step + 2][0] >= VECTOR_SORTS:
-                sort(groups[step + 2][0], groups[step + 2][1], nc.scalar.copy)
+        nc.tensor.matmul(out=bias_spread[:], lhsT=ones[:], rhs=bias_row[:], start=True, stop=True)
+        front(2, sums_pool, "acc")
+        sort(*groups[3], nc.scalar.copy, (1, 2,))
+        quantise(*groups[0])
+        nc.vector.tensor_copy(out=bias[:], in_=bias_spread[:])
+        multiply(0)
+        multiply(1)
+        sort(*groups[4], nc.scalar.copy)
+        quantise(*groups[1])
+        sort(*groups[3], nc.vector.tensor_copy, (0,))
+        multiply(2)
+        multiply(3)
+        finish(0, 0)
+        quantise(*groups[2])
+        finish(0, 1)
+        front(3)
+        sort(*groups[5], nc.scalar.copy)
+        multiply(4)
+        multiply(5)
+        finish(1, 0)
+        multiply(6)
+        finish(1, 1)
+        multiply(7)
+        for step in range(4, count + 2):
+            if step < count:
+                front(step)
+            if step + 2 < count:
+                sort(*groups[step + 2], nc.scalar.copy)
             made = []
-            if 0 <= step - 1 < count:
-                lo, hi = groups[step - 1]
-                quantise(lo, hi)
-                made = list(range(lo, hi))
-            if step == 1:
-                nc.vector.tensor_copy(out=bias[:], in_=bias_spread[:])
+            if step - 1 < count:
+                quantise(*groups[step - 1])
+                made = list(range(*groups[step - 1]))
             for j in made[:2]:
                 multiply(j)
-            if 0 <= step - 2 < count:
-                lo, hi = groups[step - 2]
-                half = (lo + hi) // 2
-                for n, j in enumerate(range(lo, hi)):
-                    add_bias(j)
-                    if n + 2 < len(made):
-                        multiply(made[n + 2])
-                    if step - 2 == count - 1 and j >= half:
-                        relu_vector(j, j + 1)
-                    elif (step - 2 >= 2 and n in SCALAR_RELUS[hi - lo]) or (step - 2 >= LATE and j >= half) or step - 2 == count - 1:
-                        relu_scalar(j, j + 1)
-                    else:
-                        relu_gpsimd(j, j + 1)
-                    if hi - lo == 2:
-                        store(j, j + 1)
-                    elif n % 2 == 1:
-                        store(j - 1, j + 1)
-            else:
-                for j in made[2:]:
-                    multiply(j)
+            for n in range(groups[step - 2][1] - groups[step - 2][0]):
+                finish(step - 2, n)
+                if n + 2 < len(made):
+                    multiply(made[n + 2])

@@ -56,7 +56,7 @@ def tile_edgemodel_pa_kernel(
         w_scales = keep.tile([P, LATENT], U8, align_bytes=64)
         ones = keep.tile([P, P], BF16)
         bias_row = keep.tile([P, LATENT], BF16)
-        bias = keep.tile([P, LATENT], F32)
+        bias = keep.tile([P, LATENT], BF16)
         global_values = keep.tile([P, 4], BF16)
         table_warmer = keep.tile([P, 1], F32)
         loaded = [
@@ -168,8 +168,6 @@ def tile_edgemodel_pa_kernel(
         nc.scalar.activation(out=table_warmer[:], in_=table_warmer[:], func=ACT.Relu)
         nc.vector.memset(ones[:], 1.0)
         nc.vector.memset(x_words[:, :, 2 * OWN :], 0.0)
-        prefill(0, nc.vector.tensor_copy)
-        prefill(1, nc.vector.tensor_copy)
         prefill(2, nc.scalar.copy)
         prefill(3, nc.scalar.copy)
 
@@ -186,11 +184,13 @@ def tile_edgemodel_pa_kernel(
                 store(j + 1 - k, j + 1)
 
         sort(0, 2, nc.vector.tensor_copy)
-        sort(2, 4, nc.vector.tensor_copy)
         front(0)
-        sort(4, 8, nc.vector.tensor_copy)
+        sort(2, 4, nc.vector.tensor_copy)
         front(1)
-        bias_spread = sums_pool.tile([P, LATENT], F32, name="acc")
+        prefill(0, nc.vector.tensor_copy)
+        sort(4, 8, nc.vector.tensor_copy)
+        prefill(1, nc.vector.tensor_copy)
+        bias_spread = sums_pool.tile([P, LATENT], BF16, name="acc")
         nc.tensor.matmul(out=bias_spread[:], lhsT=ones[:], rhs=bias_row[:], start=True, stop=True)
         front(2, sums_pool, "acc")
         sort(*groups[3], nc.scalar.copy, (1, 2,))

@@ -24,7 +24,7 @@ SLOTS = 4
 OWN = 3 * QUADRANT
 LARGEST_F32 = 3.4028234663852886e38
 GROUP_SIZES = (2, 2, 4, 4, 4, 4, 4, 4, 2, 2)
-LOADS = ((0, 4), (4, 8), (8, 12), (12, 16), (16, 24), (24, 32))
+LOADS = ((0, 4), (4, 8), (8, 12), (12, 16), (16, 20), (20, 32))
 LATE = 5
 
 VECTOR_SORTS = 8
@@ -138,10 +138,22 @@ def tile_edgemodel_pa_kernel(
         def relu_vector(lo, hi):
             nc.vector.tensor_scalar_max(out=result[:, lo:hi, :], in0=result[:, lo:hi, :], scalar1=0.0)
 
+        def relu_halves(lo, hi):
+            mid = LATENT // 2
+            nc.scalar.activation(out=result[:, lo:hi, :mid], in_=result[:, lo:hi, :mid], func=ACT.Relu)
+            nc.gpsimd.tensor_scalar(
+                out=result[:, lo:hi, mid:],
+                in0=result[:, lo:hi, mid:],
+                scalar1=LARGEST_F32,
+                scalar2=0.0,
+                op0=ALU.min,
+                op1=ALU.max,
+            )
+
         def relu(group, n, j):
             size = groups[group][1] - groups[group][0]
-            pat = "GG" if group < 2 else "SV" if group == count - 1 else "GS" if size == 2 else "GGSS" if group >= 6 else "GGSG"
-            {"G": relu_gpsimd, "S": relu_scalar, "V": relu_vector}[pat[n]](j, j + 1)
+            pat = "GG" if group == 0 else "GS" if group == 1 else "HH" if group == count - 1 else "HH" if size == 2 else "HHHH" if group >= 6 else "GGSG"
+            {"G": relu_gpsimd, "S": relu_scalar, "V": relu_vector, "H": relu_halves}[pat[n]](j, j + 1)
 
         def store(lo, hi):
             nc.sync.dma_start(out=out_rows[:, lo:hi, :], in_=result[:, lo:hi, :])

import concourse.mybir as mybir
from concourse.masks import make_identity

FLOPS = 2 * 4096 * 512 * 512

BF16 = mybir.dt.bfloat16
F32 = mybir.dt.float32
I32 = mybir.dt.int32
U8 = mybir.dt.uint8
U32 = mybir.dt.uint32
FP8X4 = mybir.dt.float8_e4m3fn_x4
FP4X4 = mybir.dt.float4_e2m1fn_x4
ALU = mybir.AluOpType
ACT = mybir.ActivationFunctionType

P = 128
EDGES = 4096
TILES = EDGES // P
FEATURES = 128
QUADRANT = FEATURES // 4
LATENT = 512
PAIR = 2
SLOTS = 4
OWN = 3 * QUADRANT
LARGEST_F32 = 3.4028234663852886e38
GROUP_SIZES = (2, 2, 4, 4, 4, 4, 4, 4, 2, 2)
LOADS = ((0, 4), (4, 8), (8, 12), (12, 16), (16, 20), (20, 32))
LATE = 5

VECTOR_SORTS = 8


def tile_edgemodel_pa_kernel(
    tc, receiver, sender, edge_attr, global_attr, W1_words, W1_scales, b1, out
):
    nc = tc.nc
    streams = [
        piece.rearrange("(p j) k -> p j k", j=TILES) for piece in (receiver, sender, edge_attr)
    ]
    out_rows = out.rearrange("(p j) n -> p j n", j=TILES)
    groups = []
    first = 0
    for size in GROUP_SIZES:
        groups.append((first, first + size))
        first += size
    count = len(groups)

    with (
        tc.tile_pool(name="keep", bufs=1) as keep,
        tc.psum_pool(name="planes", bufs=2) as planes_pool,
        tc.psum_pool(name="sums", bufs=6) as sums_pool,
        tc.manual_schedule(),
    ):
        identity = keep.tile([P, P], F32)
        w_words = keep.tile([P, 2 * LATENT], U8, align_bytes=64)
        w_scales = keep.tile([P, LATENT], U8, align_bytes=64)
        ones = keep.tile([P, P], BF16)
        bias_row = keep.tile([P, LATENT], BF16)
        bias = keep.tile([P, LATENT], BF16)
        global_values = keep.tile([P, 4], BF16)
        table_warmer = keep.tile([P, 1], F32)
        loaded = [
            keep.tile([P, TILES, FEATURES], BF16, name="loaded_%d" % s) for s in range(len(streams))
        ]
        x_words = keep.tile([P, TILES, 2 * OWN + QUADRANT], F32)
        x_grouped = keep.tile([P, SLOTS, PAIR, 4 * P], BF16, align_bytes=64)
        x_codes = keep.tile([P, TILES, P], U32, align_bytes=64)
        x_scales = keep.tile([P, TILES, P], U8, align_bytes=64)
        result = keep.tile([P, TILES, LATENT], F32)
        sums = {}

        def load(lo, hi):
            for s, stream in enumerate(streams):
                nc.sync.dma_start(out=loaded[s][:, lo:hi, :], in_=stream[:, lo:hi, :])

        def sort(lo, hi, copy, pieces=range(3)):
            for s in pieces:
                copy(
                    out=x_words[:, lo:hi, : 2 * OWN].rearrange("p j (u q) -> p j u q", u=2)[
                        :, :, :, s * QUADRANT : (s + 1) * QUADRANT
                    ],
                    in_=loaded[s][:, lo:hi, :].bitcast(F32).rearrange("p j (q u) -> p j u q", u=2),
                )

        def prefill(slot, copy):
            copy(
                out=x_grouped[OWN:, slot].bitcast(F32).rearrange("p j (e u) -> p (j e) u", u=2),
                in_=global_values[OWN:, :].bitcast(F32).unsqueeze(1).to_broadcast([QUADRANT, PAIR * P, 2]),
            )

        def transpose_pair(i, pool, name):
            planes = pool.tile([P, PAIR, 2, P], F32, name=name)
            for jj in range(PAIR):
                for u in range(2):
                    nc.tensor.transpose(planes[:, jj, u, :], x_words[:, i * PAIR + jj, u * OWN : u * OWN + P], identity[:])
            nc.scalar.copy(
                out=x_grouped[:OWN, i % SLOTS, :, :].bitcast(F32).rearrange("p j (e u) -> p j e u", u=2),
                in_=planes[:OWN].rearrange("p j u e -> p j e u"),
            )

        def quantise(lo, hi):
            slot = (lo // PAIR) % SLOTS
            nc.vector.quantize_mx(
                out=x_codes[:, lo:hi, :].rearrange("p j e -> p (j e)").bitcast(FP8X4),
                scales=x_scales[:, lo:hi, :].rearrange("p j e -> p (j e)"),
                in_=x_grouped[:, slot : slot + (hi - lo) // PAIR, :, :].rearrange("p r j c -> p (r j c)"),
            )

        def multiply(j):
            acc = sums_pool.tile([P, LATENT], F32)
            nc.tensor.matmul_mx(
                out=acc[:],
                lhsT=x_codes[:, j, :].bitcast(FP8X4),
                lhsT_scale=x_scales[:, j, :],
                rhs=w_words[:].bitcast(FP4X4),
                rhs_scale=w_scales[:],
                start=True,
                stop=True,
            )
            sums[j] = acc

        def add_bias(j):
            nc.vector.tensor_tensor(out=result[:, j, :], in0=sums[j][:], in1=bias[:], op=ALU.add)

        def relu_gpsimd(lo, hi):
            nc.gpsimd.tensor_scalar(
                out=result[:, lo:hi, :],
                in0=result[:, lo:hi, :],
                scalar1=LARGEST_F32,
                scalar2=0.0,
                op0=ALU.min,
                op1=ALU.max,
            )

        def relu_scalar(lo, hi):
            nc.scalar.activation(out=result[:, lo:hi, :], in_=result[:, lo:hi, :], func=ACT.Relu)

        def relu_vector(lo, hi):
            nc.vector.tensor_scalar_max(out=result[:, lo:hi, :], in0=result[:, lo:hi, :], scalar1=0.0)

        def relu_halves(lo, hi):
            mid = LATENT // 2
            nc.scalar.activation(out=result[:, lo:hi, :mid], in_=result[:, lo:hi, :mid], func=ACT.Relu)
            nc.gpsimd.tensor_scalar(
                out=result[:, lo:hi, mid:],
                in0=result[:, lo:hi, mid:],
                scalar1=LARGEST_F32,
                scalar2=0.0,
                op0=ALU.min,
                op1=ALU.max,
            )

        def relu(group, n, j):
            size = groups[group][1] - groups[group][0]
            pat = "GG" if group == 0 else "GS" if group == 1 else "HH" if group == count - 1 else "HH" if size == 2 else "HHHH" if group >= 6 else "GGSG"
            {"G": relu_gpsimd, "S": relu_scalar, "V": relu_vector, "H": relu_halves}[pat[n]](j, j + 1)

        def store(lo, hi):
            nc.sync.dma_start(out=out_rows[:, lo:hi, :], in_=result[:, lo:hi, :])

        nc.vector.memset(bias_row[:], 0.0)
        nc.scalar.dma_start(
            out=global_values[OWN:, :], in_=global_attr.rearrange("o (q t) -> (o q) t", t=4)
        )
        nc.scalar.dma_start(out=bias_row[0:1, :], in_=b1.rearrange("(o n) -> o n", o=1))
        load(*LOADS[0])
        load(*LOADS[1])
        nc.sync.dma_start(out=w_words[:].bitcast(I32), in_=W1_words[0].bitcast(I32))
        nc.vector.memset(w_scales[:].bitcast(I32), 0)
        for quadrant in range(4):
            nc.sync.dma_start(
                out=w_scales[32 * quadrant : 32 * quadrant + 4, :].bitcast(I32),
                in_=W1_scales[0, 4 * quadrant : 4 * quadrant + 4, :].bitcast(I32),
            )
        for lo, hi in LOADS[2:]:
            load(lo, hi)

        make_identity(nc, identity[:])
        nc.vector.memset(table_warmer[:], 0.0)
        nc.scalar.activation(out=table_warmer[:], in_=table_warmer[:], func=ACT.Relu)
        nc.vector.memset(ones[:], 1.0)
        nc.vector.memset(x_words[:, :, 2 * OWN :], 0.0)
        prefill(2, nc.scalar.copy)
        prefill(3, nc.scalar.copy)

        def front(group, pool=planes_pool, name="planes"):
            for i in range(groups[group][0] // PAIR, groups[group][1] // PAIR):
                transpose_pair(i, pool, name)

        def finish(group, n):
            j = groups[group][0] + n
            add_bias(j)
            relu(group, n, j)
            k = [2,2,2,2,2,2,2,2,2,2][group]
            if (n + 1) % k == 0:
                store(j + 1 - k, j + 1)

        sort(0, 2, nc.vector.tensor_copy)
        front(0)
        sort(2, 4, nc.vector.tensor_copy)
        front(1)
        prefill(0, nc.vector.tensor_copy)
        sort(4, 8, nc.vector.tensor_copy)
        prefill(1, nc.vector.tensor_copy)
        bias_spread = sums_pool.tile([P, LATENT], BF16, name="acc")
        nc.tensor.matmul(out=bias_spread[:], lhsT=ones[:], rhs=bias_row[:], start=True, stop=True)
        front(2, sums_pool, "acc")
        sort(*groups[3], nc.scalar.copy, (1, 2,))
        quantise(*groups[0])
        nc.vector.tensor_copy(out=bias[:], in_=bias_spread[:])
        multiply(0)
        multiply(1)
        sort(*groups[4], nc.scalar.copy)
        quantise(*groups[1])
        sort(*groups[3], nc.vector.tensor_copy, (0,))
        multiply(2)
        multiply(3)
        finish(0, 0)
        quantise(*groups[2])
        finish(0, 1)
        front(3)
        sort(*groups[5], nc.scalar.copy)
        multiply(4)
        multiply(5)
        finish(1, 0)
        multiply(6)
        finish(1, 1)
        multiply(7)
        for step in range(4, count + 2):
            if step < count:
                front(step)
            if step + 2 < count:
                sort(*groups[step + 2], nc.scalar.copy)
            made = []
            if step - 1 < count:
                quantise(*groups[step - 1])
                made = list(range(*groups[step - 1]))
            for j in made[:2]:
                multiply(j)
            for n in range(groups[step - 2][1] - groups[step - 2][0]):
                finish(step - 2, n)
                if n + 2 < len(made):
                    multiply(made[n + 2])
